import numpy as np
import ml_dtypes


def mxq(x, axis, fmt="e4m3"):
    dtype, down = {"e4m3": (ml_dtypes.float8_e4m3fn, 7), "e5m2": (ml_dtypes.float8_e5m2, 14)}[fmt]
    v = np.moveaxis(np.asarray(x, np.float32).astype(ml_dtypes.bfloat16).astype(np.float64), axis, -1)
    blocks = v.reshape(v.shape[:-1] + (-1, 32))
    amax = np.abs(blocks).max(-1, keepdims=True)
    byte = np.maximum(np.where(amax > 0, np.frexp(amax)[1] - 1 + 127, 0) - down, 1)
    scale = np.exp2(byte - 127.0)
    codes = (blocks / scale).astype(np.float32).astype(dtype).astype(np.float64)
    return np.moveaxis((codes * scale).reshape(v.shape), -1, axis)


WIDE = False


def mx_kscale(k):
    if not WIDE:
        return np.ones(k)
    levels = np.array([10, -10, 5, -5, 0])
    a = np.random.permutation(np.resize(levels, k // 512 * 4)).reshape(k // 512, 4)
    idx = np.arange(k)
    return np.exp2(a[idx // 512, idx % 128 // 32])


BF16 = ml_dtypes.bfloat16


def bf(x):
    return np.asarray(x, np.float32).astype(BF16)


def f64(x):
    return np.asarray(x).astype(np.float64)


N, IN_DIM, HID, OUT_DIM = 8192, 1024, 512, 128
CAT = 3 * HID


def log_softmax(v):
    d = v - v.max(-1, keepdims=True)
    return d - np.log(np.exp(d).sum(-1, keepdims=True))


def setup_inputs():
    s, t = mx_kscale(HID), mx_kscale(CAT)
    ta, tb, tc = t[:HID], t[HID:2 * HID], t[2 * HID:]
    return {"u1": bf(np.maximum(np.random.standard_normal((N, HID)) * 2.0, 0.0) * s),
            "W2_1": bf(np.random.standard_normal((HID, HID)) * 0.5 / np.sqrt(HID) / s[:, None] * tc),
            "b2_1": bf(np.random.standard_normal(HID) * 0.3 * tc),
            "h": bf(np.random.standard_normal((N, HID)) * ta),
            "h1": bf(np.random.standard_normal((N, HID)) * 0.8 * tb),
            "W_out": bf(np.random.standard_normal((CAT, OUT_DIM)) * 2.0 / np.sqrt(CAT) / t[:, None]),
            "b_out": bf(np.random.standard_normal(OUT_DIM) * 0.3)}


def reference(u1, W2_1, b2_1, h, h1, W_out, b_out):
    h2 = (mxq(f64(u1), 1, "e4m3") @ mxq(f64(W2_1), 0, "e4m3")) + f64(b2_1)
    cat = np.concatenate([f64(h), f64(h1), h2], axis=-1)
    logits = (mxq(cat, 1, "e4m3") @ mxq(f64(W_out), 0, "e4m3")) + f64(b_out)
    return log_softmax(logits)

@@ -1,0 +1,320 @@
+from contextlib import ExitStack
+
+import concourse.bass as bass
+import concourse.mybir as mybir
+import concourse.tile as tile
+from concourse.masks import make_identity
+
+F32 = mybir.dt.float32
+BF16 = mybir.dt.bfloat16
+U32 = mybir.dt.uint32
+U8 = mybir.dt.uint8
+FP8X4 = mybir.dt.float8_e4m3fn_x4
+ALU = mybir.AluOpType
+ACT = mybir.ActivationFunctionType
+AX = mybir.AxisListType
+
+P = 128
+NODES = 8192
+HID = 512
+OUT_DIM = 128
+TILES = NODES // P
+TPS = 4
+STEPS = TILES // TPS
+SN = TPS * P
+LOOKAHEAD = 5
+FLOPS = 2 * NODES * (HID * HID + 3 * HID * OUT_DIM)
+
+
+def tile_gin_pc_t_kernel(tc, u1, W2_1, b2_1, h, h1, W_out, b_out, out):
+    nc = tc.nc
+    with ExitStack() as ctx:
+        const = ctx.enter_context(tc.tile_pool(name="const", bufs=1))
+        inp = ctx.enter_context(tc.tile_pool(name="inp", bufs=LOOKAHEAD))
+        grp = ctx.enter_context(tc.tile_pool(name="grp", bufs=3))
+        cod = ctx.enter_context(tc.tile_pool(name="cod", bufs=3))
+        psum = ctx.enter_context(tc.psum_pool(name="psum", bufs=1))
+        ctx.enter_context(tc.manual_schedule())
+
+        srcs = {
+            "u": u1.rearrange("(p j) k -> p (j k)", j=TILES),
+            "h": h.rearrange("(p j) k -> p (j k)", j=TILES),
+            "g": h1.rearrange("(p j) k -> p (j k)", j=TILES),
+        }
+        out_v = out.rearrange("(p j) c -> p (j c)", j=TILES)
+        raw = {}
+        grouped = {}
+        codes = {}
+
+        def load(s):
+            xu = inp.tile([P, TPS * HID], BF16)
+            xh = inp.tile([P, TPS * HID], BF16)
+            xg = inp.tile([P, TPS * HID], BF16)
+            cols = slice(s * TPS * HID, (s + 1) * TPS * HID)
+            nc.sync.dma_start(out=xu[:], in_=srcs["u"][:, cols])
+            nc.sync.dma_start(out=xh[:], in_=srcs["h"][:, cols])
+            nc.sync.dma_start(out=xg[:], in_=srcs["g"][:, cols])
+            raw["u", s] = xu
+            raw["h", s] = xh
+            raw["g", s] = xg
+
+        load(0)
+        w2raw = const.tile([P, 4 * HID], BF16)
+        for u in range(2):
+            nc.sync.dma_start(
+                out=w2raw[:, u * 2 * HID:(u + 1) * 2 * HID],
+                in_=W2_1[256 * u:256 * (u + 1), :].rearrange("(q e) c -> q (e c)", e=2),
+            )
+        zb2 = const.tile([P, P], BF16)
+        zbo = const.tile([P, 2 * P], BF16)
+        ones = const.tile([P, P], BF16)
+        nc.vector.memset(zb2[:], 0.0)
+        nc.vector.memset(zbo[:], 0.0)
+        nc.vector.memset(ones[:], 1.0)
+        nc.scalar.dma_start(out=zb2[0:4, :], in_=b2_1.rearrange("(t p) -> t p", p=P))
+        nc.scalar.dma_start(out=zbo[0:1, 0:P], in_=b_out.rearrange("(o c) -> o c", o=1))
+        woraw = const.tile([P, 3 * 4 * OUT_DIM], BF16)
+        for g in range(2):
+            for u in range(2):
+                nc.scalar.dma_start(
+                    out=woraw[:, g * 512 + u * 256:g * 512 + (u + 1) * 256],
+                    in_=W_out[512 * g + 256 * u:512 * g + 256 * (u + 1), :].rearrange(
+                        "(q e) c -> q (e c)", e=2
+                    ),
+                )
+        nc.scalar.dma_start(
+            out=woraw[:, 1024:1536].rearrange("p (t c) -> p t c", t=4),
+            in_=W_out[1024:1536, :].rearrange("(t p) c -> p t c", p=P),
+        )
+        load(1)
+        load(2)
+
+        ident = const.tile([P, P], F32)
+        make_identity(nc, ident[:])
+        ident_bf = const.tile([P, P], BF16)
+        nc.vector.tensor_copy(out=ident_bf[:], in_=ident[:])
+
+        w2g = const.tile([P, 4 * HID], BF16, align_bytes=64)
+        w2c = const.tile([P, HID], U32, align_bytes=64)
+        w2s = const.tile([P, HID], U8, align_bytes=64)
+        nc.vector.tensor_copy(
+            out=w2g[:].rearrange("p (c t) -> p c t", t=4),
+            in_=w2raw[:].rearrange("p (t c) -> p c t", t=4),
+        )
+        wog = const.tile([P, 3 * 4 * OUT_DIM], BF16, align_bytes=64)
+        woc = const.tile([P, 3 * OUT_DIM], U32, align_bytes=64)
+        wos = const.tile([P, 3 * OUT_DIM], U8, align_bytes=64)
+        for g in range(3):
+            nc.vector.tensor_copy(
+                out=wog[:, g * 512:(g + 1) * 512].rearrange("p (c t) -> p c t", t=4),
+                in_=woraw[:, g * 512:(g + 1) * 512].rearrange("p (t c) -> p c t", t=4),
+            )
+        nc.vector.quantize_mx(out=w2c[:].bitcast(FP8X4), scales=w2s[:], in_=w2g[:])
+        for g in range(3):
+            nc.vector.quantize_mx(
+                out=woc[:, g * P:(g + 1) * P].bitcast(FP8X4),
+                scales=wos[:, g * P:(g + 1) * P],
+                in_=wog[:, g * 512:(g + 1) * 512],
+            )
+
+        b2 = const.tile([P, 4], F32)
+        negb = const.tile([P, OUT_DIM], F32)
+        pz = psum.tile([P, P], BF16, tag="xt", bufs=3)
+        nc.tensor.transpose(pz[:], zb2[:], ident_bf[:])
+        nc.vector.tensor_copy(out=b2[:], in_=pz[:, 0:4])
+        pb = psum.tile([P, 2 * P], F32, tag="xt", bufs=3)
+        nc.tensor.matmul(pb[:], lhsT=ones[:], rhs=zbo[:], start=True, stop=True)
+        nc.vector.tensor_scalar(
+            out=negb[:], in0=pb[:, 0:P], scalar1=-1.0, scalar2=None, op0=ALU.mult
+        )
+
+        lneg = const.tile([P, TILES * OUT_DIM], F32)
+        mneg = const.tile([P, TILES], F32)
+        ssum = const.tile([P, TILES], F32)
+        lse = const.tile([P, TILES], F32)
+        cfin = const.tile([P, TILES], F32)
+
+        def transposes(s):
+            gu = grp.tile([P, 4 * SN], BF16, align_bytes=64)
+            gh = grp.tile([P, 8 * SN], BF16, align_bytes=64)
+            grouped["u", s] = gu
+            grouped["h", s] = gh
+            for key, dst, base in (("u", gu, 0), ("h", gh, 0), ("g", gh, 2 * SN)):
+                words = raw[key, s][:].bitcast(F32)
+                dst_w = dst[:].bitcast(F32)
+                for b in range(2):
+                    xt = psum.tile([P, 2, 2 * P], F32, tag="xt", bufs=3)
+                    for j2 in range(2):
+                        j = 2 * b + j2
+                        for u in range(2):
+                            nc.tensor.transpose(
+                                xt[:, u, j2 * P:(j2 + 1) * P],
+                                words[:, j * 256 + u * P:j * 256 + (u + 1) * P],
+                                ident[:],
+                            )
+                    nc.scalar.copy(
+                        out=dst_w[:, base + b * 512:base + (b + 1) * 512].rearrange(
+                            "p (n u) -> p n u", u=2
+                        ),
+                        in_=xt[:].rearrange("p u n -> p n u"),
+                    )
+
+        def quant_u(s):
+            cu = cod.tile([P, SN], U32, align_bytes=64)
+            su = cod.tile([P, SN], U8, align_bytes=64)
+            nc.vector.quantize_mx(out=cu[:].bitcast(FP8X4), scales=su[:], in_=grouped["u", s][:])
+            codes["u", s] = (cu, su)
+
+        def quant_h(s):
+            ch = cod.tile([P, 2 * SN], U32, align_bytes=64)
+            sh = cod.tile([P, 2 * SN], U8, align_bytes=64)
+            nc.vector.quantize_mx(out=ch[:].bitcast(FP8X4), scales=sh[:], in_=grouped["h", s][:])
+            codes["h", s] = (ch, sh)
+
+        def mx1(s):
+            cu, su = codes["u", s]
+            g2 = grp.tile([P, 4 * SN], BF16, align_bytes=64)
+            planes = grp.tile([P, 4 * 2 * P], BF16)
+            grouped["2", s] = g2
+            for b in range(2):
+                hq = psum.tile([P, 512], F32, tag="h2p", bufs=4)
+                for tt in range(2):
+                    t = 2 * b + tt
+                    nc.tensor.matmul_mx(
+                        out=hq[:, tt * 256:(tt + 1) * 256],
+                        lhsT=w2c[:, t * P:(t + 1) * P].bitcast(FP8X4),
+                        lhsT_scale=w2s[:, t * P:(t + 1) * P],
+                        rhs=cu[:, 256:512].bitcast(FP8X4),
+                        rhs_scale=su[:, 256:512],
+                        start=True,
+                        stop=True,
+                    )
+                for tt in range(2):
+                    t = 2 * b + tt
+                    nc.scalar.activation(
+                        out=planes[:, t * 256:(t + 1) * 256],
+                        in_=hq[:, tt * 256:(tt + 1) * 256],
+                        func=ACT.Identity,
+                        bias=b2[:, t:t + 1],
+                        scale=1.0,
+                    )
+            for j in range(2):
+                hp = psum.tile([P, 512], F32, tag="h2p", bufs=4)
+                for t in range(4):
+                    nc.tensor.matmul_mx(
+                        out=hp[:, t * P:(t + 1) * P],
+                        lhsT=w2c[:, t * P:(t + 1) * P].bitcast(FP8X4),
+                        lhsT_scale=w2s[:, t * P:(t + 1) * P],
+                        rhs=cu[:, j * P:(j + 1) * P].bitcast(FP8X4),
+                        rhs_scale=su[:, j * P:(j + 1) * P],
+                        start=True,
+                        stop=True,
+                    )
+                nc.vector.tensor_tensor(
+                    out=g2[:, j * 512:(j + 1) * 512].rearrange("p (n t) -> p n t", t=4),
+                    in0=hp[:].rearrange("p (t n) -> p n t", t=4),
+                    in1=b2[:].unsqueeze(1).to_broadcast([P, P, 4]),
+                    op=ALU.add,
+                )
+            return planes
+
+        def regroup(s, planes):
+            g2 = grouped["2", s]
+            nc.vector.tensor_copy(
+                out=g2[:, 1024:2048].rearrange("p (c i t) -> p c t i", i=4, t=4),
+                in_=planes[:].rearrange("p (t c i) -> p c t i", t=4, i=4),
+            )
+
+        def quant_2(s):
+            c2 = cod.tile([P, SN], U32, align_bytes=64)
+            s2 = cod.tile([P, SN], U8, align_bytes=64)
+            nc.vector.quantize_mx(out=c2[:].bitcast(FP8X4), scales=s2[:], in_=grouped["2", s][:])
+            codes["2", s] = (c2, s2)
+
+        def mx2(s):
+            ch, sh = codes["h", s]
+            c2, s2 = codes["2", s]
+            lp = psum.tile([P, TPS * OUT_DIM], F32, tag="lp", bufs=1)
+            for j in range(TPS):
+                ops = (
+                    (ch, sh, j * P),
+                    (ch, sh, SN + j * P),
+                    (c2, s2, j * P),
+                )
+                for g in range(3):
+                    cc, ss, c0 = ops[g]
+                    nc.tensor.matmul_mx(
+                        out=lp[:, j * OUT_DIM:(j + 1) * OUT_DIM],
+                        lhsT=cc[:, c0:c0 + P].bitcast(FP8X4),
+                        lhsT_scale=ss[:, c0:c0 + P],
+                        rhs=woc[:, g * P:(g + 1) * P].bitcast(FP8X4),
+                        rhs_scale=wos[:, g * P:(g + 1) * P],
+                        start=(g == 0),
+                        stop=(g == 2),
+                    )
+            return lp
+
+        def logits(s, lp):
+            cols = slice(s * TPS * OUT_DIM, (s + 1) * TPS * OUT_DIM)
+            nc.vector.tensor_tensor(
+                out=lneg[:, cols].rearrange("p (j c) -> p j c", j=TPS),
+                in0=negb[:].unsqueeze(1).to_broadcast([P, TPS, OUT_DIM]),
+                in1=lp[:].rearrange("p (j c) -> p j c", j=TPS),
+                op=ALU.subtract,
+            )
+            nc.vector.tensor_reduce(
+                out=mneg[:, s * TPS:(s + 1) * TPS],
+                in_=lneg[:, cols].rearrange("p (j c) -> p j c", j=TPS),
+                axis=AX.X,
+                op=ALU.min,
+            )
+
+        def exps(s):
+            for j in range(s * TPS, (s + 1) * TPS):
+                junk = grp.tile([P, OUT_DIM], BF16)
+                nc.scalar.activation(
+                    out=junk[:],
+                    in_=lneg[:, j * OUT_DIM:(j + 1) * OUT_DIM],
+                    func=ACT.Exp,
+                    bias=mneg[:, j:j + 1],
+                    scale=-1.0,
+                    accum_out=ssum[:, j:j + 1],
+                )
+
+        def finish(j0, j1):
+            nc.scalar.activation(out=lse[:, j0:j1], in_=ssum[:, j0:j1], func=ACT.Ln)
+            nc.vector.tensor_tensor(
+                out=cfin[:, j0:j1], in0=mneg[:, j0:j1], in1=lse[:, j0:j1], op=ALU.subtract
+            )
+            for a in range(j0, j1, 8):
+                cols = slice(a * OUT_DIM, (a + 8) * OUT_DIM)
+                nc.vector.tensor_tensor(
+                    out=lneg[:, cols].rearrange("p (j c) -> p j c", j=8),
+                    in0=cfin[:, a:a + 8].unsqueeze(2).to_broadcast([P, 8, OUT_DIM]),
+                    in1=lneg[:, cols].rearrange("p (j c) -> p j c", j=8),
+                    op=ALU.subtract,
+                )
+                nc.sync.dma_start(out=out_v[:, cols], in_=lneg[:, cols])
+
+        for i in range(-2, STEPS + 2):
+            if 3 <= i + LOOKAHEAD < STEPS:
+                load(i + LOOKAHEAD)
+            planes = None
+            if 0 <= i < STEPS:
+                planes = mx1(i)
+            if 0 <= i + 1 < STEPS:
+                quant_u(i + 1)
+            if 0 <= i < STEPS:
+                regroup(i, planes)
+            if 0 <= i + 1 < STEPS:
+                quant_h(i + 1)
+            if 0 <= i < STEPS:
+                quant_2(i)
+            if 0 <= i - 1 < STEPS:
+                lp = mx2(i - 1)
+                logits(i - 1, lp)
+            if 0 <= i - 2 < STEPS:
+                exps(i - 2)
+            if 0 <= i + 2 < STEPS:
+                transposes(i + 2)
+        finish(0, TILES)

@@ -47,12 +47,12 @@ def tile_gin_pc_t_kernel(tc, u1, W2_1, b2_1, h, h1, W_out, b_out, out):
         codes = {}
 
         def load(s):
-            xu = inp.tile([P, TPS * HID], BF16)
-            xh = inp.tile([P, TPS * HID], BF16)
-            xg = inp.tile([P, TPS * HID], BF16)
             cols = slice(s * TPS * HID, (s + 1) * TPS * HID)
+            xu = inp.tile([P, TPS * HID], BF16)
             nc.sync.dma_start(out=xu[:], in_=srcs["u"][:, cols])
+            xh = inp.tile([P, TPS * HID], BF16)
             nc.sync.dma_start(out=xh[:], in_=srcs["h"][:, cols])
+            xg = inp.tile([P, TPS * HID], BF16)
             nc.sync.dma_start(out=xg[:], in_=srcs["g"][:, cols])
             raw["u", s] = xu
             raw["h", s] = xh
@@ -119,14 +119,15 @@ def tile_gin_pc_t_kernel(tc, u1, W2_1, b2_1, h, h1, W_out, b_out, out):
 
         b2 = const.tile([P, 4], F32)
         negb = const.tile([P, OUT_DIM], F32)
-        pz = psum.tile([P, P], BF16, tag="xt", bufs=3)
-        nc.tensor.transpose(pz[:], zb2[:], ident_bf[:])
-        nc.vector.tensor_copy(out=b2[:], in_=pz[:, 0:4])
-        pb = psum.tile([P, 2 * P], F32, tag="xt", bufs=3)
-        nc.tensor.matmul(pb[:], lhsT=ones[:], rhs=zbo[:], start=True, stop=True)
-        nc.vector.tensor_scalar(
-            out=negb[:], in0=pb[:, 0:P], scalar1=-1.0, scalar2=None, op0=ALU.mult
-        )
+        def bias_setup():
+            pz = psum.tile([P, P], BF16, tag="ps", bufs=8)
+            nc.tensor.transpose(pz[:], zb2[:], ident_bf[:])
+            nc.vector.tensor_copy(out=b2[:], in_=pz[:, 0:4])
+            pb = psum.tile([P, 2 * P], F32, tag="ps", bufs=8)
+            nc.tensor.matmul(pb[:], lhsT=ones[:], rhs=zbo[:], start=True, stop=True)
+            nc.vector.tensor_scalar(
+                out=negb[:], in0=pb[:, 0:P], scalar1=-1.0, scalar2=None, op0=ALU.mult
+            )
 
         lneg = const.tile([P, TILES * OUT_DIM], F32)
         mneg = const.tile([P, TILES], F32)
@@ -134,30 +135,35 @@ def tile_gin_pc_t_kernel(tc, u1, W2_1, b2_1, h, h1, W_out, b_out, out):
         lse = const.tile([P, TILES], F32)
         cfin = const.tile([P, TILES], F32)
 
-        def transposes(s):
-            gu = grp.tile([P, 4 * SN], BF16, align_bytes=64)
-            gh = grp.tile([P, 8 * SN], BF16, align_bytes=64)
-            grouped["u", s] = gu
-            grouped["h", s] = gh
-            for key, dst, base in (("u", gu, 0), ("h", gh, 0), ("g", gh, 2 * SN)):
-                words = raw[key, s][:].bitcast(F32)
-                dst_w = dst[:].bitcast(F32)
-                for b in range(2):
-                    xt = psum.tile([P, 2, 2 * P], F32, tag="xt", bufs=3)
-                    for j2 in range(2):
-                        j = 2 * b + j2
-                        for u in range(2):
-                            nc.tensor.transpose(
-                                xt[:, u, j2 * P:(j2 + 1) * P],
-                                words[:, j * 256 + u * P:j * 256 + (u + 1) * P],
-                                ident[:],
-                            )
-                    nc.scalar.copy(
-                        out=dst_w[:, base + b * 512:base + (b + 1) * 512].rearrange(
-                            "p (n u) -> p n u", u=2
-                        ),
-                        in_=xt[:].rearrange("p u n -> p n u"),
+        banks = {}
+
+        def t_pe(s, key, b):
+            if ("u", s) not in grouped:
+                gu = grp.tile([P, 4 * SN], BF16, align_bytes=64)
+                gh = grp.tile([P, 8 * SN], BF16, align_bytes=64)
+                grouped["u", s] = gu
+                grouped["h", s] = gh
+            words = raw[key, s][:].bitcast(F32)
+            xt = psum.tile([P, 512], F32, tag="ps", bufs=8)
+            banks[key, b, s] = xt
+            for j2 in range(2):
+                j = 2 * b + j2
+                for u in range(2):
+                    nc.tensor.transpose(
+                        xt[:, u * 256 + j2 * P:u * 256 + (j2 + 1) * P],
+                        words[:, j * 256 + u * P:j * 256 + (u + 1) * P],
+                        ident[:],
                     )
+
+        def t_copy(s, key, b):
+            dst = grouped["u" if key == "u" else "h", s]
+            base = 2 * SN if key == "g" else 0
+            nc.scalar.copy(
+                out=dst[:].bitcast(F32)[:, base + b * 512:base + (b + 1) * 512].rearrange(
+                    "p (n u) -> p n u", u=2
+                ),
+                in_=banks[key, b, s][:].rearrange("p (u n) -> p n u", u=2),
+            )
 
         def quant_u(s):
             cu = cod.tile([P, SN], U32, align_bytes=64)
@@ -171,13 +177,15 @@ def tile_gin_pc_t_kernel(tc, u1, W2_1, b2_1, h, h1, W_out, b_out, out):
             nc.vector.quantize_mx(out=ch[:].bitcast(FP8X4), scales=sh[:], in_=grouped["h", s][:])
             codes["h", s] = (ch, sh)
 
-        def mx1(s):
+        def mx1_planes(s):
             cu, su = codes["u", s]
             g2 = grp.tile([P, 4 * SN], BF16, align_bytes=64)
             planes = grp.tile([P, 4 * 2 * P], BF16)
             grouped["2", s] = g2
+            grouped["p", s] = planes
             for b in range(2):
-                hq = psum.tile([P, 512], F32, tag="h2p", bufs=4)
+                hq = psum.tile([P, 512], F32, tag="ps", bufs=8)
+                banks["q", b, s] = hq
                 for tt in range(2):
                     t = 2 * b + tt
                     nc.tensor.matmul_mx(
@@ -189,17 +197,23 @@ def tile_gin_pc_t_kernel(tc, u1, W2_1, b2_1, h, h1, W_out, b_out, out):
                         start=True,
                         stop=True,
                     )
+            for b in range(2):
                 for tt in range(2):
                     t = 2 * b + tt
                     nc.scalar.activation(
                         out=planes[:, t * 256:(t + 1) * 256],
-                        in_=hq[:, tt * 256:(tt + 1) * 256],
+                        in_=banks["q", b, s][:, tt * 256:(tt + 1) * 256],
                         func=ACT.Identity,
                         bias=b2[:, t:t + 1],
                         scale=1.0,
                     )
+
+        def mx1_direct(s):
+            cu, su = codes["u", s]
+            g2 = grouped["2", s]
             for j in range(2):
-                hp = psum.tile([P, 512], F32, tag="h2p", bufs=4)
+                hp = psum.tile([P, 512], F32, tag="ps", bufs=8)
+                banks["d", j, s] = hp
                 for t in range(4):
                     nc.tensor.matmul_mx(
                         out=hp[:, t * P:(t + 1) * P],
@@ -210,19 +224,18 @@ def tile_gin_pc_t_kernel(tc, u1, W2_1, b2_1, h, h1, W_out, b_out, out):
                         start=True,
                         stop=True,
                     )
+            for j in range(2):
                 nc.vector.tensor_tensor(
                     out=g2[:, j * 512:(j + 1) * 512].rearrange("p (n t) -> p n t", t=4),
-                    in0=hp[:].rearrange("p (t n) -> p n t", t=4),
+                    in0=banks["d", j, s][:].rearrange("p (t n) -> p n t", t=4),
                     in1=b2[:].unsqueeze(1).to_broadcast([P, P, 4]),
                     op=ALU.add,
                 )
-            return planes
 
-        def regroup(s, planes):
-            g2 = grouped["2", s]
+        def regroup(s):
             nc.vector.tensor_copy(
-                out=g2[:, 1024:2048].rearrange("p (c i t) -> p c t i", i=4, t=4),
-                in_=planes[:].rearrange("p (t c i) -> p c t i", t=4, i=4),
+                out=grouped["2", s][:, 1024:2048].rearrange("p (c i t) -> p c t i", i=4, t=4),
+                in_=grouped["p", s][:].rearrange("p (t c i) -> p c t i", t=4, i=4),
             )
 
         def quant_2(s):
@@ -234,13 +247,9 @@ def tile_gin_pc_t_kernel(tc, u1, W2_1, b2_1, h, h1, W_out, b_out, out):
         def mx2(s):
             ch, sh = codes["h", s]
             c2, s2 = codes["2", s]
-            lp = psum.tile([P, TPS * OUT_DIM], F32, tag="lp", bufs=1)
+            lp = psum.tile([P, 512], F32, tag="ps", bufs=8)
             for j in range(TPS):
-                ops = (
-                    (ch, sh, j * P),
-                    (ch, sh, SN + j * P),
-                    (c2, s2, j * P),
-                )
+                ops = ((ch, sh, j * P), (ch, sh, SN + j * P), (c2, s2, j * P))
                 for g in range(3):
                     cc, ss, c0 = ops[g]
                     nc.tensor.matmul_mx(
@@ -252,9 +261,6 @@ def tile_gin_pc_t_kernel(tc, u1, W2_1, b2_1, h, h1, W_out, b_out, out):
                         start=(g == 0),
                         stop=(g == 2),
                     )
-            return lp
-
-        def logits(s, lp):
             cols = slice(s * TPS * OUT_DIM, (s + 1) * TPS * OUT_DIM)
             nc.vector.tensor_tensor(
                 out=lneg[:, cols].rearrange("p (j c) -> p j c", j=TPS),
@@ -262,6 +268,9 @@ def tile_gin_pc_t_kernel(tc, u1, W2_1, b2_1, h, h1, W_out, b_out, out):
                 in1=lp[:].rearrange("p (j c) -> p j c", j=TPS),
                 op=ALU.subtract,
             )
+
+        def row_min(s):
+            cols = slice(s * TPS * OUT_DIM, (s + 1) * TPS * OUT_DIM)
             nc.vector.tensor_reduce(
                 out=mneg[:, s * TPS:(s + 1) * TPS],
                 in_=lneg[:, cols].rearrange("p (j c) -> p j c", j=TPS),
@@ -286,35 +295,57 @@ def tile_gin_pc_t_kernel(tc, u1, W2_1, b2_1, h, h1, W_out, b_out, out):
             nc.vector.tensor_tensor(
                 out=cfin[:, j0:j1], in0=mneg[:, j0:j1], in1=lse[:, j0:j1], op=ALU.subtract
             )
-            for a in range(j0, j1, 8):
-                cols = slice(a * OUT_DIM, (a + 8) * OUT_DIM)
+            for a in range(j0, j1, 4):
+                cols = slice(a * OUT_DIM, (a + 4) * OUT_DIM)
                 nc.vector.tensor_tensor(
-                    out=lneg[:, cols].rearrange("p (j c) -> p j c", j=8),
-                    in0=cfin[:, a:a + 8].unsqueeze(2).to_broadcast([P, 8, OUT_DIM]),
-                    in1=lneg[:, cols].rearrange("p (j c) -> p j c", j=8),
+                    out=lneg[:, cols].rearrange("p (j c) -> p j c", j=4),
+                    in0=cfin[:, a:a + 4].unsqueeze(2).to_broadcast([P, 4, OUT_DIM]),
+                    in1=lneg[:, cols].rearrange("p (j c) -> p j c", j=4),
                     op=ALU.subtract,
                 )
-                nc.sync.dma_start(out=out_v[:, cols], in_=lneg[:, cols])
+                if a % 8 == 4:
+                    both = slice((a - 4) * OUT_DIM, (a + 4) * OUT_DIM)
+                    nc.sync.dma_start(out=out_v[:, both], in_=lneg[:, both])
+
+        def live(s):
+            return 0 <= s < STEPS
 
         for i in range(-2, STEPS + 2):
             if 3 <= i + LOOKAHEAD < STEPS:
                 load(i + LOOKAHEAD)
-            planes = None
-            if 0 <= i < STEPS:
-                planes = mx1(i)
-            if 0 <= i + 1 < STEPS:
+            if live(i):
+                mx1_planes(i)
+            if live(i + 2):
+                t_pe(i + 2, "u", 0)
+                t_pe(i + 2, "u", 1)
+                t_copy(i + 2, "u", 0)
+                t_copy(i + 2, "u", 1)
+            if live(i + 1):
                 quant_u(i + 1)
-            if 0 <= i < STEPS:
-                regroup(i, planes)
-            if 0 <= i + 1 < STEPS:
-                quant_h(i + 1)
-            if 0 <= i < STEPS:
-                quant_2(i)
-            if 0 <= i - 1 < STEPS:
-                lp = mx2(i - 1)
-                logits(i - 1, lp)
-            if 0 <= i - 2 < STEPS:
+            if live(i):
+                mx1_direct(i)
+            if live(i - 2):
                 exps(i - 2)
-            if 0 <= i + 2 < STEPS:
-                transposes(i + 2)
+            if live(i + 2):
+                t_pe(i + 2, "h", 0)
+                t_pe(i + 2, "h", 1)
+                t_copy(i + 2, "h", 0)
+                t_copy(i + 2, "h", 1)
+            if live(i + 1):
+                quant_h(i + 1)
+            if live(i):
+                regroup(i)
+            if live(i - 1):
+                mx2(i - 1)
+            if live(i + 2):
+                t_pe(i + 2, "g", 0)
+                t_pe(i + 2, "g", 1)
+                t_copy(i + 2, "g", 0)
+                t_copy(i + 2, "g", 1)
+            if live(i):
+                quant_2(i)
+            if live(i - 1):
+                row_min(i - 1)
+            if i == -2:
+                bias_setup()
         finish(0, TILES)

@@ -1,8 +1,6 @@
 from contextlib import ExitStack
 
-import concourse.bass as bass
 import concourse.mybir as mybir
-import concourse.tile as tile
 from concourse.masks import make_identity
 
 F32 = mybir.dt.float32
@@ -22,7 +20,7 @@ TILES = NODES // P
 TPS = 4
 STEPS = TILES // TPS
 SN = TPS * P
-LOOKAHEAD = 5
+BANK = 512
 FLOPS = 2 * NODES * (HID * HID + 3 * HID * OUT_DIM)
 
 
@@ -30,10 +28,10 @@ def tile_gin_pc_t_kernel(tc, u1, W2_1, b2_1, h, h1, W_out, b_out, out):
     nc = tc.nc
     with ExitStack() as ctx:
         const = ctx.enter_context(tc.tile_pool(name="const", bufs=1))
-        inp = ctx.enter_context(tc.tile_pool(name="inp", bufs=LOOKAHEAD))
-        grp = ctx.enter_context(tc.tile_pool(name="grp", bufs=3))
+        inp = ctx.enter_context(tc.tile_pool(name="inp", bufs=4))
+        grp = ctx.enter_context(tc.tile_pool(name="grp", bufs=2))
         cod = ctx.enter_context(tc.tile_pool(name="cod", bufs=3))
-        psum = ctx.enter_context(tc.psum_pool(name="psum", bufs=1))
+        psum = ctx.enter_context(tc.psum_pool(name="psum", bufs=8))
         ctx.enter_context(tc.manual_schedule())
 
         srcs = {
@@ -45,49 +43,46 @@ def tile_gin_pc_t_kernel(tc, u1, W2_1, b2_1, h, h1, W_out, b_out, out):
         raw = {}
         grouped = {}
         codes = {}
+        banks = {}
 
-        def load(s):
-            cols = slice(s * TPS * HID, (s + 1) * TPS * HID)
-            xu = inp.tile([P, TPS * HID], BF16)
-            nc.sync.dma_start(out=xu[:], in_=srcs["u"][:, cols])
-            xh = inp.tile([P, TPS * HID], BF16)
-            nc.sync.dma_start(out=xh[:], in_=srcs["h"][:, cols])
-            xg = inp.tile([P, TPS * HID], BF16)
-            nc.sync.dma_start(out=xg[:], in_=srcs["g"][:, cols])
-            raw["u", s] = xu
-            raw["h", s] = xh
-            raw["g", s] = xg
+        def load(key, s):
+            x = inp.tile([P, TPS * HID], BF16, tag="x" + key)
+            nc.sync.dma_start(out=x[:], in_=srcs[key][:, s * TPS * HID:(s + 1) * TPS * HID])
+            raw[key, s] = x
 
-        load(0)
         w2raw = const.tile([P, 4 * HID], BF16)
         for u in range(2):
             nc.sync.dma_start(
                 out=w2raw[:, u * 2 * HID:(u + 1) * 2 * HID],
                 in_=W2_1[256 * u:256 * (u + 1), :].rearrange("(q e) c -> q (e c)", e=2),
             )
+        load("u", 0)
+        load("u", 1)
+        load("h", 0)
+        load("g", 0)
+        load("u", 2)
+        woraw = const.tile([P, 3 * 4 * OUT_DIM], BF16)
+        for a in range(4):
+            nc.sync.dma_start(
+                out=woraw[:, a * 256:(a + 1) * 256],
+                in_=W_out[256 * a:256 * (a + 1), :].rearrange("(q e) c -> q (e c)", e=2),
+            )
+        nc.sync.dma_start(
+            out=woraw[:, 1024:1536].rearrange("p (t c) -> p t c", t=4),
+            in_=W_out[1024:1536, :].rearrange("(t p) c -> p t c", p=P),
+        )
+
         zb2 = const.tile([P, P], BF16)
         zbo = const.tile([P, 2 * P], BF16)
         ones = const.tile([P, P], BF16)
+        warm = const.tile([P, 2], F32)
+        nc.vector.memset(warm[:], 0.0)
         nc.vector.memset(zb2[:], 0.0)
         nc.vector.memset(zbo[:], 0.0)
         nc.vector.memset(ones[:], 1.0)
         nc.scalar.dma_start(out=zb2[0:4, :], in_=b2_1.rearrange("(t p) -> t p", p=P))
         nc.scalar.dma_start(out=zbo[0:1, 0:P], in_=b_out.rearrange("(o c) -> o c", o=1))
-        woraw = const.tile([P, 3 * 4 * OUT_DIM], BF16)
-        for g in range(2):
-            for u in range(2):
-                nc.scalar.dma_start(
-                    out=woraw[:, g * 512 + u * 256:g * 512 + (u + 1) * 256],
-                    in_=W_out[512 * g + 256 * u:512 * g + 256 * (u + 1), :].rearrange(
-                        "(q e) c -> q (e c)", e=2
-                    ),
-                )
-        nc.scalar.dma_start(
-            out=woraw[:, 1024:1536].rearrange("p (t c) -> p t c", t=4),
-            in_=W_out[1024:1536, :].rearrange("(t p) c -> p t c", p=P),
-        )
-        load(1)
-        load(2)
+        nc.scalar.activation(out=warm[:, 1:2], in_=warm[:, 0:1], func=ACT.Exp)
 
         ident = const.tile([P, P], F32)
         make_identity(nc, ident[:])
@@ -98,36 +93,40 @@ def tile_gin_pc_t_kernel(tc, u1, W2_1, b2_1, h, h1, W_out, b_out, out):
         w2c = const.tile([P, HID], U32, align_bytes=64)
         w2s = const.tile([P, HID], U8, align_bytes=64)
         nc.vector.tensor_copy(
-            out=w2g[:].rearrange("p (c t) -> p c t", t=4),
-            in_=w2raw[:].rearrange("p (t c) -> p c t", t=4),
+            out=w2g[:].rearrange("p (c i t) -> p c t i", i=4, t=4),
+            in_=w2raw[:].rearrange("p (t c i) -> p c t i", t=4, i=4),
         )
         wog = const.tile([P, 3 * 4 * OUT_DIM], BF16, align_bytes=64)
         woc = const.tile([P, 3 * OUT_DIM], U32, align_bytes=64)
         wos = const.tile([P, 3 * OUT_DIM], U8, align_bytes=64)
-        for g in range(3):
-            nc.vector.tensor_copy(
-                out=wog[:, g * 512:(g + 1) * 512].rearrange("p (c t) -> p c t", t=4),
-                in_=woraw[:, g * 512:(g + 1) * 512].rearrange("p (t c) -> p c t", t=4),
-            )
-        nc.vector.quantize_mx(out=w2c[:].bitcast(FP8X4), scales=w2s[:], in_=w2g[:])
-        for g in range(3):
-            nc.vector.quantize_mx(
-                out=woc[:, g * P:(g + 1) * P].bitcast(FP8X4),
-                scales=wos[:, g * P:(g + 1) * P],
-                in_=wog[:, g * 512:(g + 1) * 512],
-            )
-
         b2 = const.tile([P, 4], F32)
         negb = const.tile([P, OUT_DIM], F32)
+
+        def w2_quant():
+            nc.vector.quantize_mx(out=w2c[:].bitcast(FP8X4), scales=w2s[:], in_=w2g[:])
+
         def bias_setup():
-            pz = psum.tile([P, P], BF16, tag="ps", bufs=8)
+            pz = psum.tile([P, P], BF16, tag="ps")
             nc.tensor.transpose(pz[:], zb2[:], ident_bf[:])
             nc.vector.tensor_copy(out=b2[:], in_=pz[:, 0:4])
-            pb = psum.tile([P, 2 * P], F32, tag="ps", bufs=8)
+            pb = psum.tile([P, 2 * P], F32, tag="ps")
             nc.tensor.matmul(pb[:], lhsT=ones[:], rhs=zbo[:], start=True, stop=True)
             nc.vector.tensor_scalar(
                 out=negb[:], in0=pb[:, 0:P], scalar1=-1.0, scalar2=None, op0=ALU.mult
             )
+
+        def wout_setup():
+            for g in range(3):
+                nc.vector.tensor_copy(
+                    out=wog[:, g * 512:(g + 1) * 512].rearrange("p (c t) -> p c t", t=4),
+                    in_=woraw[:, g * 512:(g + 1) * 512].rearrange("p (t c) -> p c t", t=4),
+                )
+            for g in range(3):
+                nc.vector.quantize_mx(
+                    out=woc[:, g * P:(g + 1) * P].bitcast(FP8X4),
+                    scales=wos[:, g * P:(g + 1) * P],
+                    in_=wog[:, g * 512:(g + 1) * 512],
+                )
 
         lneg = const.tile([P, TILES * OUT_DIM], F32)
         mneg = const.tile([P, TILES], F32)
@@ -135,35 +134,36 @@ def tile_gin_pc_t_kernel(tc, u1, W2_1, b2_1, h, h1, W_out, b_out, out):
         lse = const.tile([P, TILES], F32)
         cfin = const.tile([P, TILES], F32)
 
-        banks = {}
-
-        def t_pe(s, key, b):
-            if ("u", s) not in grouped:
-                gu = grp.tile([P, 4 * SN], BF16, align_bytes=64)
-                gh = grp.tile([P, 8 * SN], BF16, align_bytes=64)
+        def transposes(s, key):
+            if key == "u":
+                gu = grp.tile([P, 4 * SN], BF16, align_bytes=64, bufs=3)
                 grouped["u", s] = gu
+            if key == "h":
+                gh = grp.tile([P, 8 * SN], BF16, align_bytes=64)
                 grouped["h", s] = gh
             words = raw[key, s][:].bitcast(F32)
-            xt = psum.tile([P, 512], F32, tag="ps", bufs=8)
-            banks[key, b, s] = xt
-            for j2 in range(2):
-                j = 2 * b + j2
-                for u in range(2):
-                    nc.tensor.transpose(
-                        xt[:, u * 256 + j2 * P:u * 256 + (j2 + 1) * P],
-                        words[:, j * 256 + u * P:j * 256 + (u + 1) * P],
-                        ident[:],
-                    )
-
-        def t_copy(s, key, b):
             dst = grouped["u" if key == "u" else "h", s]
             base = 2 * SN if key == "g" else 0
-            nc.scalar.copy(
-                out=dst[:].bitcast(F32)[:, base + b * 512:base + (b + 1) * 512].rearrange(
+            for b in range(2):
+                xt = psum.tile([P, BANK], F32, tag="ps")
+                banks[b] = xt
+                for j2 in range(2):
+                    j = 2 * b + j2
+                    for u in range(2):
+                        nc.tensor.transpose(
+                            xt[:, u * 256 + j2 * P:u * 256 + (j2 + 1) * P],
+                            words[:, j * 256 + u * P:j * 256 + (u + 1) * P],
+                            ident[:],
+                        )
+            for b in range(2):
+                dst_ap = dst[:].bitcast(F32)[:, base + b * 512:base + (b + 1) * 512].rearrange(
                     "p (n u) -> p n u", u=2
-                ),
-                in_=banks[key, b, s][:].rearrange("p (u n) -> p n u", u=2),
-            )
+                )
+                src_ap = banks[b][:].rearrange("p (u n) -> p n u", u=2)
+                if key == "g" and b == 1 and (False):
+                    nc.vector.tensor_copy(out=dst_ap, in_=src_ap)
+                else:
+                    nc.scalar.copy(out=dst_ap, in_=src_ap)
 
         def quant_u(s):
             cu = cod.tile([P, SN], U32, align_bytes=64)
@@ -172,8 +172,8 @@ def tile_gin_pc_t_kernel(tc, u1, W2_1, b2_1, h, h1, W_out, b_out, out):
             codes["u", s] = (cu, su)
 
         def quant_h(s):
-            ch = cod.tile([P, 2 * SN], U32, align_bytes=64)
-            sh = cod.tile([P, 2 * SN], U8, align_bytes=64)
+            ch = cod.tile([P, 2 * SN], U32, align_bytes=64, bufs=2)
+            sh = cod.tile([P, 2 * SN], U8, align_bytes=64, bufs=2)
             nc.vector.quantize_mx(out=ch[:].bitcast(FP8X4), scales=sh[:], in_=grouped["h", s][:])
             codes["h", s] = (ch, sh)
 
@@ -184,8 +184,8 @@ def tile_gin_pc_t_kernel(tc, u1, W2_1, b2_1, h, h1, W_out, b_out, out):
             grouped["2", s] = g2
             grouped["p", s] = planes
             for b in range(2):
-                hq = psum.tile([P, 512], F32, tag="ps", bufs=8)
-                banks["q", b, s] = hq
+                hq = psum.tile([P, BANK], F32, tag="ps")
+                banks[b] = hq
                 for tt in range(2):
                     t = 2 * b + tt
                     nc.tensor.matmul_mx(
@@ -202,7 +202,7 @@ def tile_gin_pc_t_kernel(tc, u1, W2_1, b2_1, h, h1, W_out, b_out, out):
                     t = 2 * b + tt
                     nc.scalar.activation(
                         out=planes[:, t * 256:(t + 1) * 256],
-                        in_=banks["q", b, s][:, tt * 256:(tt + 1) * 256],
+                        in_=banks[b][:, tt * 256:(tt + 1) * 256],
                         func=ACT.Identity,
                         bias=b2[:, t:t + 1],
                         scale=1.0,
@@ -212,8 +212,8 @@ def tile_gin_pc_t_kernel(tc, u1, W2_1, b2_1, h, h1, W_out, b_out, out):
             cu, su = codes["u", s]
             g2 = grouped["2", s]
             for j in range(2):
-                hp = psum.tile([P, 512], F32, tag="ps", bufs=8)
-                banks["d", j, s] = hp
+                hp = psum.tile([P, BANK], F32, tag="ps")
+                banks[j] = hp
                 for t in range(4):
                     nc.tensor.matmul_mx(
                         out=hp[:, t * P:(t + 1) * P],
@@ -227,7 +227,7 @@ def tile_gin_pc_t_kernel(tc, u1, W2_1, b2_1, h, h1, W_out, b_out, out):
             for j in range(2):
                 nc.vector.tensor_tensor(
                     out=g2[:, j * 512:(j + 1) * 512].rearrange("p (n t) -> p n t", t=4),
-                    in0=banks["d", j, s][:].rearrange("p (t n) -> p n t", t=4),
+                    in0=banks[j][:].rearrange("p (t n) -> p n t", t=4),
                     in1=b2[:].unsqueeze(1).to_broadcast([P, P, 4]),
                     op=ALU.add,
                 )
@@ -247,7 +247,7 @@ def tile_gin_pc_t_kernel(tc, u1, W2_1, b2_1, h, h1, W_out, b_out, out):
         def mx2(s):
             ch, sh = codes["h", s]
             c2, s2 = codes["2", s]
-            lp = psum.tile([P, 512], F32, tag="ps", bufs=8)
+            lp = psum.tile([P, BANK], F32, tag="ps")
             for j in range(TPS):
                 ops = ((ch, sh, j * P), (ch, sh, SN + j * P), (c2, s2, j * P))
                 for g in range(3):
@@ -295,7 +295,7 @@ def tile_gin_pc_t_kernel(tc, u1, W2_1, b2_1, h, h1, W_out, b_out, out):
             nc.vector.tensor_tensor(
                 out=cfin[:, j0:j1], in0=mneg[:, j0:j1], in1=lse[:, j0:j1], op=ALU.subtract
             )
-            for a in range(j0, j1, 4):
+            for a in range(j0, j1, 8):
                 cols = slice(a * OUT_DIM, (a + 4) * OUT_DIM)
                 nc.vector.tensor_tensor(
                     out=lneg[:, cols].rearrange("p (j c) -> p j c", j=4),
@@ -303,49 +303,51 @@ def tile_gin_pc_t_kernel(tc, u1, W2_1, b2_1, h, h1, W_out, b_out, out):
                     in1=lneg[:, cols].rearrange("p (j c) -> p j c", j=4),
                     op=ALU.subtract,
                 )
-                if a % 8 == 4:
-                    both = slice((a - 4) * OUT_DIM, (a + 4) * OUT_DIM)
-                    nc.sync.dma_start(out=out_v[:, both], in_=lneg[:, both])
+                for j in range(a + 4, a + 8):
+                    nc.scalar.activation(
+                        out=lneg[:, j * OUT_DIM:(j + 1) * OUT_DIM],
+                        in_=lneg[:, j * OUT_DIM:(j + 1) * OUT_DIM],
+                        func=ACT.Identity,
+                        bias=cfin[:, j:j + 1],
+                        scale=-1.0,
+                    )
+                both = slice(a * OUT_DIM, (a + 8) * OUT_DIM)
+                nc.sync.dma_start(out=out_v[:, both], in_=lneg[:, both])
 
         def live(s):
             return 0 <= s < STEPS
 
         for i in range(-2, STEPS + 2):
-            if 3 <= i + LOOKAHEAD < STEPS:
-                load(i + LOOKAHEAD)
+            if live(i + 3) and i + 3 >= 1:
+                load("h", i + 3)
+                load("g", i + 3)
+            if live(i + 5) and i + 5 >= 3:
+                load("u", i + 5)
+            if live(i - 1):
+                quant_h(i - 1)
             if live(i):
                 mx1_planes(i)
             if live(i + 2):
-                t_pe(i + 2, "u", 0)
-                t_pe(i + 2, "u", 1)
-                t_copy(i + 2, "u", 0)
-                t_copy(i + 2, "u", 1)
+                transposes(i + 2, "u")
+            if i == -2:
+                w2_quant()
+                bias_setup()
             if live(i + 1):
                 quant_u(i + 1)
             if live(i):
                 mx1_direct(i)
+            if i == 0:
+                wout_setup()
             if live(i - 2):
                 exps(i - 2)
-            if live(i + 2):
-                t_pe(i + 2, "h", 0)
-                t_pe(i + 2, "h", 1)
-                t_copy(i + 2, "h", 0)
-                t_copy(i + 2, "h", 1)
-            if live(i + 1):
-                quant_h(i + 1)
             if live(i):
+                transposes(i, "h")
                 regroup(i)
             if live(i - 1):
                 mx2(i - 1)
-            if live(i + 2):
-                t_pe(i + 2, "g", 0)
-                t_pe(i + 2, "g", 1)
-                t_copy(i + 2, "g", 0)
-                t_copy(i + 2, "g", 1)
             if live(i):
+                transposes(i, "g")
                 quant_2(i)
             if live(i - 1):
                 row_min(i - 1)
-            if i == -2:
-                bias_setup()
         finish(0, TILES)

@@ -290,20 +290,16 @@ def tile_gin_pc_t_kernel(tc, u1, W2_1, b2_1, h, h1, W_out, b_out, out):
                     accum_out=ssum[:, j:j + 1],
                 )
 
-        def finish(j0, j1):
+        def log_sums(j0, j1):
             nc.scalar.activation(out=lse[:, j0:j1], in_=ssum[:, j0:j1], func=ACT.Ln)
             nc.vector.tensor_tensor(
                 out=cfin[:, j0:j1], in0=mneg[:, j0:j1], in1=lse[:, j0:j1], op=ALU.subtract
             )
-            for a in range(j0, j1, 8):
-                cols = slice(a * OUT_DIM, (a + 4) * OUT_DIM)
-                nc.vector.tensor_tensor(
-                    out=lneg[:, cols].rearrange("p (j c) -> p j c", j=4),
-                    in0=cfin[:, a:a + 4].unsqueeze(2).to_broadcast([P, 4, OUT_DIM]),
-                    in1=lneg[:, cols].rearrange("p (j c) -> p j c", j=4),
-                    op=ALU.subtract,
-                )
-                for j in range(a + 4, a + 8):
+
+        def results(on_scalar, j0, j1):
+            cols = slice(j0 * OUT_DIM, j1 * OUT_DIM)
+            if on_scalar:
+                for j in range(j0, j1):
                     nc.scalar.activation(
                         out=lneg[:, j * OUT_DIM:(j + 1) * OUT_DIM],
                         in_=lneg[:, j * OUT_DIM:(j + 1) * OUT_DIM],
@@ -311,8 +307,14 @@ def tile_gin_pc_t_kernel(tc, u1, W2_1, b2_1, h, h1, W_out, b_out, out):
                         bias=cfin[:, j:j + 1],
                         scale=-1.0,
                     )
-                both = slice(a * OUT_DIM, (a + 8) * OUT_DIM)
-                nc.sync.dma_start(out=out_v[:, both], in_=lneg[:, both])
+            else:
+                nc.vector.tensor_tensor(
+                    out=lneg[:, cols].rearrange("p (j c) -> p j c", j=j1 - j0),
+                    in0=cfin[:, j0:j1].unsqueeze(2).to_broadcast([P, j1 - j0, OUT_DIM]),
+                    in1=lneg[:, cols].rearrange("p (j c) -> p j c", j=j1 - j0),
+                    op=ALU.subtract,
+                )
+            nc.sync.dma_start(out=out_v[:, cols], in_=lneg[:, cols])
 
         def live(s):
             return 0 <= s < STEPS
@@ -340,6 +342,10 @@ def tile_gin_pc_t_kernel(tc, u1, W2_1, b2_1, h, h1, W_out, b_out, out):
                 wout_setup()
             if live(i - 2):
                 exps(i - 2)
+            if i - 2 == STEPS - 2:
+                log_sums(0, TILES - TPS)
+                for j0 in (0, 4, 8):
+                    results(True, j0, j0 + 4)
             if live(i):
                 transposes(i, "h")
                 regroup(i)
@@ -350,4 +356,8 @@ def tile_gin_pc_t_kernel(tc, u1, W2_1, b2_1, h, h1, W_out, b_out, out):
                 quant_2(i)
             if live(i - 1):
                 row_min(i - 1)
-        finish(0, TILES)
+            if i - 2 == STEPS - 2:
+                for j0, j1 in ((12, 16), (16, 24), (24, 32), (32, 40), (40, 48), (48, 56), (56, 60)):
+                    results(False, j0, j1)
+        log_sums(TILES - TPS, TILES)
+        results(False, TILES - TPS, TILES)

@@ -160,7 +160,7 @@ def tile_gin_pc_t_kernel(tc, u1, W2_1, b2_1, h, h1, W_out, b_out, out):
                     "p (n u) -> p n u", u=2
                 )
                 src_ap = banks[b][:].rearrange("p (u n) -> p n u", u=2)
-                if key == "g" and b == 1 and (False):
+                if key == "g" and b == 1 and (s % 2 == 0):
                     nc.vector.tensor_copy(out=dst_ap, in_=src_ap)
                 else:
                     nc.scalar.copy(out=dst_ap, in_=src_ap)
@@ -233,10 +233,19 @@ def tile_gin_pc_t_kernel(tc, u1, W2_1, b2_1, h, h1, W_out, b_out, out):
                 )
 
         def regroup(s):
-            nc.vector.tensor_copy(
-                out=grouped["2", s][:, 1024:2048].rearrange("p (c i t) -> p c t i", i=4, t=4),
-                in_=grouped["p", s][:].rearrange("p (t c i) -> p c t i", t=4, i=4),
-            )
+            for half in range(2):
+                nc.gpsimd.tensor_scalar(
+                    out=grouped["2", s][:, 1024 + half * 512:1536 + half * 512].rearrange(
+                        "p (n t) -> p n t", t=4
+                    ),
+                    in0=grouped["p", s][:].rearrange("p (t n) -> p n t", t=4)[
+                        :, half * P:(half + 1) * P, :
+                    ],
+                    scalar1=1.0,
+                    scalar2=0.0,
+                    op0=ALU.mult,
+                    op1=ALU.add,
+                )
 
         def quant_2(s):
             c2 = cod.tile([P, SN], U32, align_bytes=64)
@@ -337,6 +346,7 @@ def tile_gin_pc_t_kernel(tc, u1, W2_1, b2_1, h, h1, W_out, b_out, out):
             if live(i + 1):
                 quant_u(i + 1)
             if live(i):
+                regroup(i)
                 mx1_direct(i)
             if i == 0:
                 wout_setup()
@@ -348,14 +358,12 @@ def tile_gin_pc_t_kernel(tc, u1, W2_1, b2_1, h, h1, W_out, b_out, out):
                     results(True, j0, j0 + 4)
             if live(i):
                 transposes(i, "h")
-                regroup(i)
             if live(i - 1):
                 mx2(i - 1)
+                row_min(i - 1)
             if live(i):
                 transposes(i, "g")
                 quant_2(i)
-            if live(i - 1):
-                row_min(i - 1)
             if i - 2 == STEPS - 2:
                 for j0, j1 in ((12, 16), (16, 24), (24, 32), (32, 40), (40, 48), (48, 56), (56, 60)):
                     results(False, j0, j1)

@@ -160,7 +160,7 @@ def tile_gin_pc_t_kernel(tc, u1, W2_1, b2_1, h, h1, W_out, b_out, out):
                     "p (n u) -> p n u", u=2
                 )
                 src_ap = banks[b][:].rearrange("p (u n) -> p n u", u=2)
-                if key == "g" and b == 1 and (s % 2 == 0):
+                if key == "g" and b == 1 and (False):
                     nc.vector.tensor_copy(out=dst_ap, in_=src_ap)
                 else:
                     nc.scalar.copy(out=dst_ap, in_=src_ap)
@@ -233,19 +233,10 @@ def tile_gin_pc_t_kernel(tc, u1, W2_1, b2_1, h, h1, W_out, b_out, out):
                 )
 
         def regroup(s):
-            for half in range(2):
-                nc.gpsimd.tensor_scalar(
-                    out=grouped["2", s][:, 1024 + half * 512:1536 + half * 512].rearrange(
-                        "p (n t) -> p n t", t=4
-                    ),
-                    in0=grouped["p", s][:].rearrange("p (t n) -> p n t", t=4)[
-                        :, half * P:(half + 1) * P, :
-                    ],
-                    scalar1=1.0,
-                    scalar2=0.0,
-                    op0=ALU.mult,
-                    op1=ALU.add,
-                )
+            nc.vector.tensor_copy(
+                out=grouped["2", s][:, 1024:2048].rearrange("p (c i t) -> p c t i", i=4, t=4),
+                in_=grouped["p", s][:].rearrange("p (t c i) -> p c t i", t=4, i=4),
+            )
 
         def quant_2(s):
             c2 = cod.tile([P, SN], U32, align_bytes=64)
@@ -343,10 +334,7 @@ def tile_gin_pc_t_kernel(tc, u1, W2_1, b2_1, h, h1, W_out, b_out, out):
             if i == -2:
                 w2_quant()
                 bias_setup()
-            if live(i + 1):
-                quant_u(i + 1)
             if live(i):
-                regroup(i)
                 mx1_direct(i)
             if i == 0:
                 wout_setup()
@@ -358,12 +346,15 @@ def tile_gin_pc_t_kernel(tc, u1, W2_1, b2_1, h, h1, W_out, b_out, out):
                     results(True, j0, j0 + 4)
             if live(i):
                 transposes(i, "h")
-            if live(i - 1):
-                mx2(i - 1)
-                row_min(i - 1)
+                regroup(i)
+            if live(i + 1):
+                quant_u(i + 1)
             if live(i):
                 transposes(i, "g")
                 quant_2(i)
+            if live(i - 1):
+                mx2(i - 1)
+                row_min(i - 1)
             if i - 2 == STEPS - 2:
                 for j0, j1 in ((12, 16), (16, 24), (24, 32), (32, 40), (40, 48), (48, 56), (56, 60)):
                     results(False, j0, j1)

@@ -329,15 +329,17 @@ def tile_gin_pc_t_kernel(tc, u1, W2_1, b2_1, h, h1, W_out, b_out, out):
                 quant_h(i - 1)
             if live(i):
                 mx1_planes(i)
+            if live(i + 1):
+                quant_u(i + 1)
+            if live(i):
+                mx1_direct(i)
+            if i == 0:
+                wout_setup()
             if live(i + 2):
                 transposes(i + 2, "u")
             if i == -2:
                 w2_quant()
                 bias_setup()
-            if live(i):
-                mx1_direct(i)
-            if i == 0:
-                wout_setup()
             if live(i - 2):
                 exps(i - 2)
             if i - 2 == STEPS - 2:
@@ -347,13 +349,12 @@ def tile_gin_pc_t_kernel(tc, u1, W2_1, b2_1, h, h1, W_out, b_out, out):
             if live(i):
                 transposes(i, "h")
                 regroup(i)
-            if live(i + 1):
-                quant_u(i + 1)
+            if live(i - 1):
+                mx2(i - 1)
             if live(i):
                 transposes(i, "g")
                 quant_2(i)
             if live(i - 1):
-                mx2(i - 1)
                 row_min(i - 1)
             if i - 2 == STEPS - 2:
                 for j0, j1 in ((12, 16), (16, 24), (24, 32), (32, 40), (40, 48), (48, 56), (56, 60)):

@@ -160,7 +160,7 @@ def tile_gin_pc_t_kernel(tc, u1, W2_1, b2_1, h, h1, W_out, b_out, out):
                     "p (n u) -> p n u", u=2
                 )
                 src_ap = banks[b][:].rearrange("p (u n) -> p n u", u=2)
-                if key == "g" and b == 1 and (False):
+                if key == "g" and b == 1 and (s % 2 == 0):
                     nc.vector.tensor_copy(out=dst_ap, in_=src_ap)
                 else:
                     nc.scalar.copy(out=dst_ap, in_=src_ap)
@@ -233,10 +233,19 @@ def tile_gin_pc_t_kernel(tc, u1, W2_1, b2_1, h, h1, W_out, b_out, out):
                 )
 
         def regroup(s):
-            nc.vector.tensor_copy(
-                out=grouped["2", s][:, 1024:2048].rearrange("p (c i t) -> p c t i", i=4, t=4),
-                in_=grouped["p", s][:].rearrange("p (t c i) -> p c t i", t=4, i=4),
-            )
+            for half in range(2):
+                nc.gpsimd.tensor_scalar(
+                    out=grouped["2", s][:, 1024 + half * 512:1536 + half * 512].rearrange(
+                        "p (n t) -> p n t", t=4
+                    ),
+                    in0=grouped["p", s][:].rearrange("p (t n) -> p n t", t=4)[
+                        :, half * P:(half + 1) * P, :
+                    ],
+                    scalar1=1.0,
+                    scalar2=0.0,
+                    op0=ALU.mult,
+                    op1=ALU.add,
+                )
 
         def quant_2(s):
             c2 = cod.tile([P, SN], U32, align_bytes=64)
@@ -332,6 +341,7 @@ def tile_gin_pc_t_kernel(tc, u1, W2_1, b2_1, h, h1, W_out, b_out, out):
             if live(i + 1):
                 quant_u(i + 1)
             if live(i):
+                regroup(i)
                 mx1_direct(i)
             if i == 0:
                 wout_setup()
@@ -348,14 +358,12 @@ def tile_gin_pc_t_kernel(tc, u1, W2_1, b2_1, h, h1, W_out, b_out, out):
                     results(True, j0, j0 + 4)
             if live(i):
                 transposes(i, "h")
-                regroup(i)
             if live(i - 1):
                 mx2(i - 1)
+                row_min(i - 1)
             if live(i):
                 transposes(i, "g")
                 quant_2(i)
-            if live(i - 1):
-                row_min(i - 1)
             if i - 2 == STEPS - 2:
                 for j0, j1 in ((12, 16), (16, 24), (24, 32), (32, 40), (40, 48), (48, 56), (56, 60)):
                     results(False, j0, j1)

from contextlib import ExitStack

import concourse.mybir as mybir
from concourse.masks import make_identity

F32 = mybir.dt.float32
BF16 = mybir.dt.bfloat16
U32 = mybir.dt.uint32
U8 = mybir.dt.uint8
FP8X4 = mybir.dt.float8_e4m3fn_x4
ALU = mybir.AluOpType
ACT = mybir.ActivationFunctionType
AX = mybir.AxisListType

P = 128
NODES = 8192
HID = 512
OUT_DIM = 128
TILES = NODES // P
TPS = 4
STEPS = TILES // TPS
SN = TPS * P
BANK = 512
FLOPS = 2 * NODES * (HID * HID + 3 * HID * OUT_DIM)


def tile_gin_pc_t_kernel(tc, u1, W2_1, b2_1, h, h1, W_out, b_out, out):
    nc = tc.nc
    with ExitStack() as ctx:
        const = ctx.enter_context(tc.tile_pool(name="const", bufs=1))
        inp = ctx.enter_context(tc.tile_pool(name="inp", bufs=4))
        grp = ctx.enter_context(tc.tile_pool(name="grp", bufs=2))
        cod = ctx.enter_context(tc.tile_pool(name="cod", bufs=3))
        psum = ctx.enter_context(tc.psum_pool(name="psum", bufs=8))
        ctx.enter_context(tc.manual_schedule())

        srcs = {
            "u": u1.rearrange("(p j) k -> p (j k)", j=TILES),
            "h": h.rearrange("(p j) k -> p (j k)", j=TILES),
            "g": h1.rearrange("(p j) k -> p (j k)", j=TILES),
        }
        out_v = out.rearrange("(p j) c -> p (j c)", j=TILES)
        raw = {}
        grouped = {}
        codes = {}
        banks = {}

        def load(key, s):
            x = inp.tile([P, TPS * HID], BF16, tag="x" + key)
            nc.sync.dma_start(out=x[:], in_=srcs[key][:, s * TPS * HID:(s + 1) * TPS * HID])
            raw[key, s] = x

        w2raw = const.tile([P, 4 * HID], BF16)
        for u in range(2):
            nc.sync.dma_start(
                out=w2raw[:, u * 2 * HID:(u + 1) * 2 * HID],
                in_=W2_1[256 * u:256 * (u + 1), :].rearrange("(q e) c -> q (e c)", e=2),
            )
        load("u", 0)
        load("u", 1)
        load("h", 0)
        load("g", 0)
        load("u", 2)
        woraw = const.tile([P, 3 * 4 * OUT_DIM], BF16)
        for a in range(4):
            nc.sync.dma_start(
                out=woraw[:, a * 256:(a + 1) * 256],
                in_=W_out[256 * a:256 * (a + 1), :].rearrange("(q e) c -> q (e c)", e=2),
            )
        nc.sync.dma_start(
            out=woraw[:, 1024:1536].rearrange("p (t c) -> p t c", t=4),
            in_=W_out[1024:1536, :].rearrange("(t p) c -> p t c", p=P),
        )

        zb2 = const.tile([P, P], BF16)
        zbo = const.tile([P, 2 * P], BF16)
        ones = const.tile([P, P], BF16)
        warm = const.tile([P, 2], F32)
        nc.vector.memset(warm[:], 0.0)
        nc.vector.memset(zb2[:], 0.0)
        nc.vector.memset(zbo[:], 0.0)
        nc.vector.memset(ones[:], 1.0)
        nc.scalar.dma_start(out=zb2[0:4, :], in_=b2_1.rearrange("(t p) -> t p", p=P))
        nc.scalar.dma_start(out=zbo[0:1, 0:P], in_=b_out.rearrange("(o c) -> o c", o=1))
        nc.scalar.activation(out=warm[:, 1:2], in_=warm[:, 0:1], func=ACT.Exp)

        ident = const.tile([P, P], F32)
        make_identity(nc, ident[:])
        ident_bf = const.tile([P, P], BF16)
        nc.vector.tensor_copy(out=ident_bf[:], in_=ident[:])

        w2g = const.tile([P, 4 * HID], BF16, align_bytes=64)
        w2c = const.tile([P, HID], U32, align_bytes=64)
        w2s = const.tile([P, HID], U8, align_bytes=64)
        nc.vector.tensor_copy(
            out=w2g[:].rearrange("p (c i t) -> p c t i", i=4, t=4),
            in_=w2raw[:].rearrange("p (t c i) -> p c t i", t=4, i=4),
        )
        wog = const.tile([P, 3 * 4 * OUT_DIM], BF16, align_bytes=64)
        woc = const.tile([P, 3 * OUT_DIM], U32, align_bytes=64)
        wos = const.tile([P, 3 * OUT_DIM], U8, align_bytes=64)
        b2 = const.tile([P, 4], F32)
        negb = const.tile([P, OUT_DIM], F32)

        def w2_quant():
            nc.vector.quantize_mx(out=w2c[:].bitcast(FP8X4), scales=w2s[:], in_=w2g[:])

        def bias_setup():
            pz = psum.tile([P, P], BF16, tag="ps")
            nc.tensor.transpose(pz[:], zb2[:], ident_bf[:])
            nc.vector.tensor_copy(out=b2[:], in_=pz[:, 0:4])
            pb = psum.tile([P, 2 * P], F32, tag="ps")
            nc.tensor.matmul(pb[:], lhsT=ones[:], rhs=zbo[:], start=True, stop=True)
            nc.vector.tensor_scalar(
                out=negb[:], in0=pb[:, 0:P], scalar1=-1.0, scalar2=None, op0=ALU.mult
            )

        def wout_setup():
            for g in range(3):
                nc.vector.tensor_copy(
                    out=wog[:, g * 512:(g + 1) * 512].rearrange("p (c t) -> p c t", t=4),
                    in_=woraw[:, g * 512:(g + 1) * 512].rearrange("p (t c) -> p c t", t=4),
                )
            for g in range(3):
                nc.vector.quantize_mx(
                    out=woc[:, g * P:(g + 1) * P].bitcast(FP8X4),
                    scales=wos[:, g * P:(g + 1) * P],
                    in_=wog[:, g * 512:(g + 1) * 512],
                )

        lneg = const.tile([P, TILES * OUT_DIM], F32)
        mneg = const.tile([P, TILES], F32)
        ssum = const.tile([P, TILES], F32)
        lse = const.tile([P, TILES], F32)
        cfin = const.tile([P, TILES], F32)

        def transposes(s, key):
            if key == "u":
                gu = grp.tile([P, 4 * SN], BF16, align_bytes=64, bufs=3)
                grouped["u", s] = gu
            if key == "h":
                gh = grp.tile([P, 8 * SN], BF16, align_bytes=64)
                grouped["h", s] = gh
            words = raw[key, s][:].bitcast(F32)
            dst = grouped["u" if key == "u" else "h", s]
            base = 2 * SN if key == "g" else 0
            for b in range(2):
                xt = psum.tile([P, BANK], F32, tag="ps")
                banks[b] = xt
                for j2 in range(2):
                    j = 2 * b + j2
                    for u in range(2):
                        nc.tensor.transpose(
                            xt[:, u * 256 + j2 * P:u * 256 + (j2 + 1) * P],
                            words[:, j * 256 + u * P:j * 256 + (u + 1) * P],
                            ident[:],
                        )
            for b in range(2):
                dst_ap = dst[:].bitcast(F32)[:, base + b * 512:base + (b + 1) * 512].rearrange(
                    "p (n u) -> p n u", u=2
                )
                src_ap = banks[b][:].rearrange("p (u n) -> p n u", u=2)
                if key == "g" and b == 1 and (s % 2 == 0):
                    nc.vector.tensor_copy(out=dst_ap, in_=src_ap)
                else:
                    nc.scalar.copy(out=dst_ap, in_=src_ap)

        def quant_u(s):
            cu = cod.tile([P, SN], U32, align_bytes=64)
            su = cod.tile([P, SN], U8, align_bytes=64)
            nc.vector.quantize_mx(out=cu[:].bitcast(FP8X4), scales=su[:], in_=grouped["u", s][:])
            codes["u", s] = (cu, su)

        def quant_h(s):
            ch = cod.tile([P, 2 * SN], U32, align_bytes=64, bufs=2)
            sh = cod.tile([P, 2 * SN], U8, align_bytes=64, bufs=2)
            nc.vector.quantize_mx(out=ch[:].bitcast(FP8X4), scales=sh[:], in_=grouped["h", s][:])
            codes["h", s] = (ch, sh)

        def mx1_planes(s):
            cu, su = codes["u", s]
            g2 = grp.tile([P, 4 * SN], BF16, align_bytes=64)
            planes = grp.tile([P, 4 * 2 * P], BF16)
            grouped["2", s] = g2
            grouped["p", s] = planes
            for b in range(2):
                hq = psum.tile([P, BANK], F32, tag="ps")
                banks[b] = hq
                for tt in range(2):
                    t = 2 * b + tt
                    nc.tensor.matmul_mx(
                        out=hq[:, tt * 256:(tt + 1) * 256],
                        lhsT=w2c[:, t * P:(t + 1) * P].bitcast(FP8X4),
                        lhsT_scale=w2s[:, t * P:(t + 1) * P],
                        rhs=cu[:, 256:512].bitcast(FP8X4),
                        rhs_scale=su[:, 256:512],
                        start=True,
                        stop=True,
                    )
            for b in range(2):
                for tt in range(2):
                    t = 2 * b + tt
                    nc.scalar.activation(
                        out=planes[:, t * 256:(t + 1) * 256],
                        in_=banks[b][:, tt * 256:(tt + 1) * 256],
                        func=ACT.Identity,
                        bias=b2[:, t:t + 1],
                        scale=1.0,
                    )

        def mx1_direct(s):
            cu, su = codes["u", s]
            g2 = grouped["2", s]
            for j in range(2):
                hp = psum.tile([P, BANK], F32, tag="ps")
                banks[j] = hp
                for t in range(4):
                    nc.tensor.matmul_mx(
                        out=hp[:, t * P:(t + 1) * P],
                        lhsT=w2c[:, t * P:(t + 1) * P].bitcast(FP8X4),
                        lhsT_scale=w2s[:, t * P:(t + 1) * P],
                        rhs=cu[:, j * P:(j + 1) * P].bitcast(FP8X4),
                        rhs_scale=su[:, j * P:(j + 1) * P],
                        start=True,
                        stop=True,
                    )
            for j in range(2):
                nc.vector.tensor_tensor(
                    out=g2[:, j * 512:(j + 1) * 512].rearrange("p (n t) -> p n t", t=4),
                    in0=banks[j][:].rearrange("p (t n) -> p n t", t=4),
                    in1=b2[:].unsqueeze(1).to_broadcast([P, P, 4]),
                    op=ALU.add,
                )

        def regroup(s):
            for half in range(2):
                nc.gpsimd.tensor_scalar(
                    out=grouped["2", s][:, 1024 + half * 512:1536 + half * 512].rearrange(
                        "p (n t) -> p n t", t=4
                    ),
                    in0=grouped["p", s][:].rearrange("p (t n) -> p n t", t=4)[
                        :, half * P:(half + 1) * P, :
                    ],
                    scalar1=1.0,
                    scalar2=0.0,
                    op0=ALU.mult,
                    op1=ALU.add,
                )

        def quant_2(s):
            c2 = cod.tile([P, SN], U32, align_bytes=64)
            s2 = cod.tile([P, SN], U8, align_bytes=64)
            nc.vector.quantize_mx(out=c2[:].bitcast(FP8X4), scales=s2[:], in_=grouped["2", s][:])
            codes["2", s] = (c2, s2)

        def mx2(s):
            ch, sh = codes["h", s]
            c2, s2 = codes["2", s]
            lp = psum.tile([P, BANK], F32, tag="ps")
            for j in range(TPS):
                ops = ((ch, sh, j * P), (ch, sh, SN + j * P), (c2, s2, j * P))
                for g in range(3):
                    cc, ss, c0 = ops[g]
                    nc.tensor.matmul_mx(
                        out=lp[:, j * OUT_DIM:(j + 1) * OUT_DIM],
                        lhsT=cc[:, c0:c0 + P].bitcast(FP8X4),
                        lhsT_scale=ss[:, c0:c0 + P],
                        rhs=woc[:, g * P:(g + 1) * P].bitcast(FP8X4),
                        rhs_scale=wos[:, g * P:(g + 1) * P],
                        start=(g == 0),
                        stop=(g == 2),
                    )
            cols = slice(s * TPS * OUT_DIM, (s + 1) * TPS * OUT_DIM)
            nc.vector.tensor_tensor(
                out=lneg[:, cols].rearrange("p (j c) -> p j c", j=TPS),
                in0=negb[:].unsqueeze(1).to_broadcast([P, TPS, OUT_DIM]),
                in1=lp[:].rearrange("p (j c) -> p j c", j=TPS),
                op=ALU.subtract,
            )

        def row_min(s):
            cols = slice(s * TPS * OUT_DIM, (s + 1) * TPS * OUT_DIM)
            nc.vector.tensor_reduce(
                out=mneg[:, s * TPS:(s + 1) * TPS],
                in_=lneg[:, cols].rearrange("p (j c) -> p j c", j=TPS),
                axis=AX.X,
                op=ALU.min,
            )

        def exps(s):
            for j in range(s * TPS, (s + 1) * TPS):
                junk = grp.tile([P, OUT_DIM], BF16)
                nc.scalar.activation(
                    out=junk[:],
                    in_=lneg[:, j * OUT_DIM:(j + 1) * OUT_DIM],
                    func=ACT.Exp,
                    bias=mneg[:, j:j + 1],
                    scale=-1.0,
                    accum_out=ssum[:, j:j + 1],
                )

        def log_sums(j0, j1):
            nc.scalar.activation(out=lse[:, j0:j1], in_=ssum[:, j0:j1], func=ACT.Ln)
            nc.vector.tensor_tensor(
                out=cfin[:, j0:j1], in0=mneg[:, j0:j1], in1=lse[:, j0:j1], op=ALU.subtract
            )

        def results(on_scalar, j0, j1):
            cols = slice(j0 * OUT_DIM, j1 * OUT_DIM)
            if on_scalar:
                for j in range(j0, j1):
                    nc.scalar.activation(
                        out=lneg[:, j * OUT_DIM:(j + 1) * OUT_DIM],
                        in_=lneg[:, j * OUT_DIM:(j + 1) * OUT_DIM],
                        func=ACT.Identity,
                        bias=cfin[:, j:j + 1],
                        scale=-1.0,
                    )
            else:
                nc.vector.tensor_tensor(
                    out=lneg[:, cols].rearrange("p (j c) -> p j c", j=j1 - j0),
                    in0=cfin[:, j0:j1].unsqueeze(2).to_broadcast([P, j1 - j0, OUT_DIM]),
                    in1=lneg[:, cols].rearrange("p (j c) -> p j c", j=j1 - j0),
                    op=ALU.subtract,
                )
            nc.sync.dma_start(out=out_v[:, cols], in_=lneg[:, cols])

        def live(s):
            return 0 <= s < STEPS

        for i in range(-2, STEPS + 2):
            if live(i + 3) and i + 3 >= 1:
                load("h", i + 3)
                load("g", i + 3)
            if live(i + 5) and i + 5 >= 3:
                load("u", i + 5)
            if live(i - 1):
                quant_h(i - 1)
            if live(i):
                mx1_planes(i)
            if live(i + 1):
                quant_u(i + 1)
            if live(i):
                regroup(i)
                mx1_direct(i)
            if i == 0:
                wout_setup()
            if live(i + 2):
                transposes(i + 2, "u")
            if i == -2:
                w2_quant()
                bias_setup()
            if live(i - 2):
                exps(i - 2)
            if i - 2 == STEPS - 2:
                log_sums(0, TILES - TPS)
                for j0 in (0, 4, 8):
                    results(True, j0, j0 + 4)
            if live(i):
                transposes(i, "h")
            if live(i - 1):
                mx2(i - 1)
                row_min(i - 1)
            if live(i):
                transposes(i, "g")
                quant_2(i)
            if i - 2 == STEPS - 2:
                for j0, j1 in ((12, 16), (16, 24), (24, 32), (32, 40), (40, 48), (48, 56), (56, 60)):
                    results(False, j0, j1)
        log_sums(TILES - TPS, TILES)
        results(False, TILES - TPS, TILES)
